import numpy as np
import ml_dtypes

BF16 = ml_dtypes.bfloat16


def bf(x):
    return np.asarray(x, np.float32).astype(BF16)


def f32(x):
    return np.asarray(x, np.float32)


def f64(x):
    return np.asarray(x).astype(np.float64)


def striped(idx):
    return np.tile(idx.reshape(-1, 16).T, (8, 1))


D, S, M, N = 128, 2048, 512, 256
DENS = 0.25


def setup_inputs():
    return {"table": bf(np.random.standard_normal((D, S))), "keys": bf(np.random.standard_normal((D, M)) / np.sqrt(D)), "mask": f32(np.random.random((M, N)) < DENS), "offs": striped(np.random.permutation(np.tile(np.arange(S), 2))[:N])}


def reference(table, keys, mask, offs):
    idx = offs[:16].T.reshape(-1)
    pos = f64(keys).T @ f64(table)[:, idx]
    return f64(mask) * (pos - 1.0) ** 2

@@ -1,0 +1,41 @@
+import concourse.mybir as mybir
+
+P = 128
+S = 2048
+M = 512
+N = 256
+KEY_BLOCKS = M // P
+
+FLOPS = 2 * P * M * N
+
+BF16, F32, U16 = mybir.dt.bfloat16, mybir.dt.float32, mybir.dt.uint16
+
+
+def tile_relationalneigborconstrastloss_kernel(tc, table, keys, mask, offs, out):
+    nc = tc.nc
+    with (
+        tc.tile_pool(name="held", bufs=1) as held,
+        tc.tile_pool(name="work", bufs=KEY_BLOCKS) as work,
+        tc.psum_pool(name="psum", bufs=KEY_BLOCKS) as psum,
+    ):
+        offsets = held.tile([P, N // 16], U16, name="offsets")
+        nc.sync.dma_start(offsets[:], offs)
+        table_sb = held.tile([P, S], BF16, name="table_sb")
+        nc.sync.dma_start(table_sb[:], table)
+        keys_sb = held.tile([P, M], BF16, name="keys_sb")
+        nc.scalar.dma_start(keys_sb[:], keys)
+
+        for b in range(KEY_BLOCKS):
+            rows = slice(b * P, (b + 1) * P)
+            mask_sb = work.tile([P, N], F32, name="mask_sb")
+            nc.scalar.dma_start(mask_sb[:], mask[rows, :])
+
+            similarity = psum.tile([P, N], F32, name="similarity")
+            nc.tensor.matmul(
+                similarity[:], keys_sb[:, rows], table_sb[:].indirect(offsets[:]), start=True, stop=True
+            )
+            squared = work.tile([P, N], F32, name="squared")
+            nc.scalar.activation(squared[:], similarity[:], mybir.ActivationFunctionType.Square, bias=-1.0)
+            result = work.tile([P, N], F32, name="result")
+            nc.vector.tensor_tensor(result[:], squared[:], mask_sb[:], mybir.AluOpType.mult)
+            nc.sync.dma_start(out[rows, :], result[:])

@@ -25,10 +25,14 @@ def tile_relationalneigborconstrastloss_kernel(tc, table, keys, mask, offs, out)
         keys_sb = held.tile([P, M], BF16, name="keys_sb")
         nc.scalar.dma_start(keys_sb[:], keys)
 
+        mask_blocks = []
+        for b in range(KEY_BLOCKS):
+            mask_sb = work.tile([P, N], F32, name="mask_sb")
+            nc.sync.dma_start(mask_sb[:], mask[b * P : (b + 1) * P, :])
+            mask_blocks.append(mask_sb)
+
         for b in range(KEY_BLOCKS):
             rows = slice(b * P, (b + 1) * P)
-            mask_sb = work.tile([P, N], F32, name="mask_sb")
-            nc.scalar.dma_start(mask_sb[:], mask[rows, :])
 
             similarity = psum.tile([P, N], F32, name="similarity")
             nc.tensor.matmul(
@@ -37,5 +41,5 @@ def tile_relationalneigborconstrastloss_kernel(tc, table, keys, mask, offs, out)
             squared = work.tile([P, N], F32, name="squared")
             nc.scalar.activation(squared[:], similarity[:], mybir.ActivationFunctionType.Square, bias=-1.0)
             result = work.tile([P, N], F32, name="result")
-            nc.vector.tensor_tensor(result[:], squared[:], mask_sb[:], mybir.AluOpType.mult)
+            nc.vector.tensor_tensor(result[:], squared[:], mask_blocks[b][:], mybir.AluOpType.mult)
             nc.sync.dma_start(out[rows, :], result[:])

@@ -5,6 +5,8 @@ S = 2048
 M = 512
 N = 256
 KEY_BLOCKS = M // P
+WARM_COLUMNS = 512
+WARM_MATMULS = 5
 
 FLOPS = 2 * P * M * N
 
@@ -17,7 +19,14 @@ def tile_relationalneigborconstrastloss_kernel(tc, table, keys, mask, offs, out)
         tc.tile_pool(name="held", bufs=1) as held,
         tc.tile_pool(name="work", bufs=KEY_BLOCKS) as work,
         tc.psum_pool(name="psum", bufs=KEY_BLOCKS) as psum,
+        tc.psum_pool(name="warm", bufs=1) as warm,
     ):
+        zeros = held.tile([P, WARM_COLUMNS], BF16, name="zeros")
+        nc.vector.memset(zeros[:], 0.0)
+        unread = warm.tile([P, WARM_COLUMNS], F32, name="unread")
+        for w in range(WARM_MATMULS):
+            nc.tensor.matmul(unread[:], zeros[:, :P], zeros[:], start=True, stop=True)
+
         offsets = held.tile([P, N // 16], U16, name="offsets")
         nc.sync.dma_start(offsets[:], offs)
         table_sb = held.tile([P, S], BF16, name="table_sb")

@@ -5,8 +5,6 @@ S = 2048
 M = 512
 N = 256
 KEY_BLOCKS = M // P
-WARM_COLUMNS = 512
-WARM_MATMULS = 5
 
 FLOPS = 2 * P * M * N
 
@@ -19,21 +17,13 @@ def tile_relationalneigborconstrastloss_kernel(tc, table, keys, mask, offs, out)
         tc.tile_pool(name="held", bufs=1) as held,
         tc.tile_pool(name="work", bufs=KEY_BLOCKS) as work,
         tc.psum_pool(name="psum", bufs=KEY_BLOCKS) as psum,
-        tc.psum_pool(name="warm", bufs=1) as warm,
     ):
-        zeros = held.tile([P, WARM_COLUMNS], BF16, name="zeros")
-        nc.vector.memset(zeros[:], 0.0)
-        unread = warm.tile([P, WARM_COLUMNS], F32, name="unread")
-        for w in range(WARM_MATMULS):
-            nc.tensor.matmul(unread[:], zeros[:, :P], zeros[:], start=True, stop=True)
-
+        table_sb = held.tile([P, S], BF16, name="table_sb")
+        nc.scalar.dma_start(table_sb[:], table)
         offsets = held.tile([P, N // 16], U16, name="offsets")
         nc.sync.dma_start(offsets[:], offs)
-        table_sb = held.tile([P, S], BF16, name="table_sb")
-        nc.sync.dma_start(table_sb[:], table)
         keys_sb = held.tile([P, M], BF16, name="keys_sb")
-        nc.scalar.dma_start(keys_sb[:], keys)
-
+        nc.sync.dma_start(keys_sb[:], keys)
         mask_blocks = []
         for b in range(KEY_BLOCKS):
             mask_sb = work.tile([P, N], F32, name="mask_sb")

@@ -10,13 +10,17 @@ FLOPS = 2 * P * M * N
 
 BF16, F32, U16 = mybir.dt.bfloat16, mybir.dt.float32, mybir.dt.uint16
 
+HALVES = 2
+PIECE = N // HALVES
+
 
 def tile_relationalneigborconstrastloss_kernel(tc, table, keys, mask, offs, out):
     nc = tc.nc
     with (
         tc.tile_pool(name="held", bufs=1) as held,
-        tc.tile_pool(name="work", bufs=KEY_BLOCKS) as work,
-        tc.psum_pool(name="psum", bufs=KEY_BLOCKS) as psum,
+        tc.tile_pool(name="mask_pool", bufs=KEY_BLOCKS) as mask_pool,
+        tc.tile_pool(name="work", bufs=KEY_BLOCKS * HALVES) as work,
+        tc.psum_pool(name="psum", bufs=KEY_BLOCKS * HALVES) as psum,
     ):
         table_sb = held.tile([P, S], BF16, name="table_sb")
         nc.scalar.dma_start(table_sb[:], table)
@@ -26,19 +30,22 @@ def tile_relationalneigborconstrastloss_kernel(tc, table, keys, mask, offs, out)
         nc.sync.dma_start(keys_sb[:], keys)
         mask_blocks = []
         for b in range(KEY_BLOCKS):
-            mask_sb = work.tile([P, N], F32, name="mask_sb")
+            mask_sb = mask_pool.tile([P, N], F32, name="mask_sb")
             nc.sync.dma_start(mask_sb[:], mask[b * P : (b + 1) * P, :])
             mask_blocks.append(mask_sb)
 
         for b in range(KEY_BLOCKS):
             rows = slice(b * P, (b + 1) * P)
+            for h in range(HALVES):
+                pairs = slice(h * PIECE, (h + 1) * PIECE)
+                piece_offsets = offsets[:, h * (PIECE // 16) : (h + 1) * (PIECE // 16)]
 
-            similarity = psum.tile([P, N], F32, name="similarity")
-            nc.tensor.matmul(
-                similarity[:], keys_sb[:, rows], table_sb[:].indirect(offsets[:]), start=True, stop=True
-            )
-            squared = work.tile([P, N], F32, name="squared")
-            nc.scalar.activation(squared[:], similarity[:], mybir.ActivationFunctionType.Square, bias=-1.0)
-            result = work.tile([P, N], F32, name="result")
-            nc.vector.tensor_tensor(result[:], squared[:], mask_blocks[b][:], mybir.AluOpType.mult)
-            nc.sync.dma_start(out[rows, :], result[:])
+                similarity = psum.tile([P, PIECE], F32, name="similarity")
+                nc.tensor.matmul(
+                    similarity[:], keys_sb[:, rows], table_sb[:].indirect(piece_offsets), start=True, stop=True
+                )
+                squared = work.tile([P, PIECE], F32, name="squared")
+                nc.scalar.activation(squared[:], similarity[:], mybir.ActivationFunctionType.Square, bias=-1.0)
+                result = work.tile([P, PIECE], F32, name="result")
+                nc.vector.tensor_tensor(result[:], squared[:], mask_blocks[b][:, pairs], mybir.AluOpType.mult)
+                nc.sync.dma_start(out[rows, pairs], result[:])

@@ -19,6 +19,7 @@ def tile_relationalneigborconstrastloss_kernel(tc, table, keys, mask, offs, out)
     with (
         tc.tile_pool(name="held", bufs=1) as held,
         tc.tile_pool(name="mask_pool", bufs=KEY_BLOCKS) as mask_pool,
+        tc.tile_pool(name="results", bufs=KEY_BLOCKS) as results,
         tc.tile_pool(name="work", bufs=KEY_BLOCKS * HALVES) as work,
         tc.psum_pool(name="psum", bufs=KEY_BLOCKS * HALVES) as psum,
     ):
@@ -36,6 +37,7 @@ def tile_relationalneigborconstrastloss_kernel(tc, table, keys, mask, offs, out)
 
         for b in range(KEY_BLOCKS):
             rows = slice(b * P, (b + 1) * P)
+            result = results.tile([P, N], F32, name="result")
             for h in range(HALVES):
                 pairs = slice(h * PIECE, (h + 1) * PIECE)
                 piece_offsets = offsets[:, h * (PIECE // 16) : (h + 1) * (PIECE // 16)]
@@ -46,6 +48,7 @@ def tile_relationalneigborconstrastloss_kernel(tc, table, keys, mask, offs, out)
                 )
                 squared = work.tile([P, PIECE], F32, name="squared")
                 nc.scalar.activation(squared[:], similarity[:], mybir.ActivationFunctionType.Square, bias=-1.0)
-                result = work.tile([P, PIECE], F32, name="result")
-                nc.vector.tensor_tensor(result[:], squared[:], mask_blocks[b][:, pairs], mybir.AluOpType.mult)
-                nc.sync.dma_start(out[rows, pairs], result[:])
+                nc.vector.tensor_tensor(
+                    result[:, pairs], squared[:], mask_blocks[b][:, pairs], mybir.AluOpType.mult
+                )
+            nc.sync.dma_start(out[rows, :], result[:])

@@ -12,12 +12,15 @@ BF16, F32, U16 = mybir.dt.bfloat16, mybir.dt.float32, mybir.dt.uint16
 
 HALVES = 2
 PIECE = N // HALVES
+KEY_LOADS = 2
+BLOCKS_PER_LOAD = KEY_BLOCKS // KEY_LOADS
 
 
 def tile_relationalneigborconstrastloss_kernel(tc, table, keys, mask, offs, out):
     nc = tc.nc
     with (
         tc.tile_pool(name="held", bufs=1) as held,
+        tc.tile_pool(name="keys_pool", bufs=KEY_LOADS) as keys_pool,
         tc.tile_pool(name="mask_pool", bufs=KEY_BLOCKS) as mask_pool,
         tc.tile_pool(name="results", bufs=KEY_BLOCKS) as results,
         tc.tile_pool(name="work", bufs=KEY_BLOCKS * HALVES) as work,
@@ -27,8 +30,11 @@ def tile_relationalneigborconstrastloss_kernel(tc, table, keys, mask, offs, out)
         nc.scalar.dma_start(table_sb[:], table)
         offsets = held.tile([P, N // 16], U16, name="offsets")
         nc.sync.dma_start(offsets[:], offs)
-        keys_sb = held.tile([P, M], BF16, name="keys_sb")
-        nc.sync.dma_start(keys_sb[:], keys)
+        keys_tiles = []
+        for t in range(KEY_LOADS):
+            keys_sb = keys_pool.tile([P, M // KEY_LOADS], BF16, name="keys_sb")
+            nc.sync.dma_start(keys_sb[:], keys[:, t * (M // KEY_LOADS) : (t + 1) * (M // KEY_LOADS)])
+            keys_tiles.append(keys_sb)
         mask_blocks = []
         for b in range(KEY_BLOCKS):
             mask_sb = mask_pool.tile([P, N], F32, name="mask_sb")
@@ -37,6 +43,8 @@ def tile_relationalneigborconstrastloss_kernel(tc, table, keys, mask, offs, out)
 
         for b in range(KEY_BLOCKS):
             rows = slice(b * P, (b + 1) * P)
+            c = b % BLOCKS_PER_LOAD
+            block_keys = keys_tiles[b // BLOCKS_PER_LOAD][:, c * P : (c + 1) * P]
             result = results.tile([P, N], F32, name="result")
             for h in range(HALVES):
                 pairs = slice(h * PIECE, (h + 1) * PIECE)
@@ -44,7 +52,7 @@ def tile_relationalneigborconstrastloss_kernel(tc, table, keys, mask, offs, out)
 
                 similarity = psum.tile([P, PIECE], F32, name="similarity")
                 nc.tensor.matmul(
-                    similarity[:], keys_sb[:, rows], table_sb[:].indirect(piece_offsets), start=True, stop=True
+                    similarity[:], block_keys, table_sb[:].indirect(piece_offsets), start=True, stop=True
                 )
                 squared = work.tile([P, PIECE], F32, name="squared")
                 nc.scalar.activation(squared[:], similarity[:], mybir.ActivationFunctionType.Square, bias=-1.0)

import concourse.mybir as mybir

P = 128
S = 2048
M = 512
N = 256
KEY_BLOCKS = M // P

FLOPS = 2 * P * M * N

BF16, F32, U16 = mybir.dt.bfloat16, mybir.dt.float32, mybir.dt.uint16

HALVES = 2
PIECE = N // HALVES
KEY_LOADS = 2
BLOCKS_PER_LOAD = KEY_BLOCKS // KEY_LOADS


def tile_relationalneigborconstrastloss_kernel(tc, table, keys, mask, offs, out):
    nc = tc.nc
    with (
        tc.tile_pool(name="held", bufs=1) as held,
        tc.tile_pool(name="keys_pool", bufs=KEY_LOADS) as keys_pool,
        tc.tile_pool(name="mask_pool", bufs=KEY_BLOCKS) as mask_pool,
        tc.tile_pool(name="results", bufs=KEY_BLOCKS) as results,
        tc.tile_pool(name="work", bufs=KEY_BLOCKS * HALVES) as work,
        tc.psum_pool(name="psum", bufs=KEY_BLOCKS * HALVES) as psum,
    ):
        table_sb = held.tile([P, S], BF16, name="table_sb")
        nc.scalar.dma_start(table_sb[:], table)
        offsets = held.tile([P, N // 16], U16, name="offsets")
        nc.sync.dma_start(offsets[:], offs)
        keys_tiles = []
        for t in range(KEY_LOADS):
            keys_sb = keys_pool.tile([P, M // KEY_LOADS], BF16, name="keys_sb")
            nc.sync.dma_start(keys_sb[:], keys[:, t * (M // KEY_LOADS) : (t + 1) * (M // KEY_LOADS)])
            keys_tiles.append(keys_sb)
        mask_blocks = []
        for b in range(KEY_BLOCKS):
            mask_sb = mask_pool.tile([P, N], F32, name="mask_sb")
            nc.sync.dma_start(mask_sb[:], mask[b * P : (b + 1) * P, :])
            mask_blocks.append(mask_sb)

        for b in range(KEY_BLOCKS):
            rows = slice(b * P, (b + 1) * P)
            c = b % BLOCKS_PER_LOAD
            block_keys = keys_tiles[b // BLOCKS_PER_LOAD][:, c * P : (c + 1) * P]
            result = results.tile([P, N], F32, name="result")
            for h in range(HALVES):
                pairs = slice(h * PIECE, (h + 1) * PIECE)
                piece_offsets = offsets[:, h * (PIECE // 16) : (h + 1) * (PIECE // 16)]

                similarity = psum.tile([P, PIECE], F32, name="similarity")
                nc.tensor.matmul(
                    similarity[:], block_keys, table_sb[:].indirect(piece_offsets), start=True, stop=True
                )
                squared = work.tile([P, PIECE], F32, name="squared")
                nc.scalar.activation(squared[:], similarity[:], mybir.ActivationFunctionType.Square, bias=-1.0)
                nc.vector.tensor_tensor(
                    result[:, pairs], squared[:], mask_blocks[b][:, pairs], mybir.AluOpType.mult
                )
            nc.sync.dma_start(out[rows, :], result[:])
